import numpy as np
import ml_dtypes


def mxq(x, axis, fmt="e4m3"):
    dtype, down = {"e4m3": (ml_dtypes.float8_e4m3fn, 7), "e5m2": (ml_dtypes.float8_e5m2, 14)}[fmt]
    v = np.moveaxis(np.asarray(x, np.float32).astype(ml_dtypes.bfloat16).astype(np.float64), axis, -1)
    blocks = v.reshape(v.shape[:-1] + (-1, 32))
    amax = np.abs(blocks).max(-1, keepdims=True)
    byte = np.maximum(np.where(amax > 0, np.frexp(amax)[1] - 1 + 127, 0) - down, 1)
    scale = np.exp2(byte - 127.0)
    codes = (blocks / scale).astype(np.float32).astype(dtype).astype(np.float64)
    return np.moveaxis((codes * scale).reshape(v.shape), -1, axis)


WIDE = False


def mx_kscale(k):
    if not WIDE:
        return np.ones(k)
    levels = np.array([10, -10, 5, -5, 0])
    a = np.random.permutation(np.resize(levels, k // 512 * 4)).reshape(k // 512, 4)
    idx = np.arange(k)
    return np.exp2(a[idx // 512, idx % 128 // 32])


BF16 = ml_dtypes.bfloat16


def bf(x):
    return np.asarray(x, np.float32).astype(BF16)


def f64(x):
    return np.asarray(x).astype(np.float64)


B, S, IN, OUT = 4, 32, 1024, 1024


def setup_inputs():
    s = mx_kscale(IN)
    w = np.random.standard_normal((OUT, IN + 1))
    w[:, :IN] *= 0.25 / np.sqrt(IN) / s
    w[:, IN] *= 0.5
    return {"x": bf(np.random.standard_normal((B, S, IN)) * s), "weight": bf(w)}


def reference(x, weight):
    w = f64(weight)
    in_features = w.shape[1] - 1
    xf = f64(x).reshape(-1, in_features)
    wm, wb = w[:, :in_features], w[:, in_features]
    xq = mxq(xf, 1, "e4m3")
    wq = mxq(wm, 1, "e4m3")
    lin = (xq @ wq.T) + wb
    ab = (np.abs(xq) @ np.abs(wq).T) + np.abs(wb)
    return 0.5 * (lin + ab)

@@ -1,0 +1,130 @@
+from contextlib import ExitStack
+
+import concourse.mybir as mybir
+from concourse.masks import make_identity
+
+F32 = mybir.dt.float32
+BF16 = mybir.dt.bfloat16
+I32 = mybir.dt.int32
+U32 = mybir.dt.uint32
+U8 = mybir.dt.uint8
+FP8X4 = mybir.dt.float8_e4m3fn_x4
+ALU = mybir.AluOpType
+ACT = mybir.ActivationFunctionType
+
+P = 128
+IN = 1024
+OUT = 1024
+PACK = 4
+PASSES = IN // (P * PACK)
+WORD_BLOCKS = IN // 2 // P
+SIGNS = 2
+UNITS = 2
+CHUNK = UNITS * P
+CHUNKS = OUT // CHUNK
+W_PITCH = 1040
+CLEAR_SIGNS = 0x7FFF7FFF
+
+FLOPS = 2 * 2 * P * IN * OUT
+
+
+def tile_skanlinear_s_kernel(tc, x, weight, out):
+    nc = tc.nc
+    x2 = x.flatten_outer_dims()
+
+    with ExitStack() as ctx:
+        const = ctx.enter_context(tc.tile_pool(name="const", bufs=1))
+        rows = ctx.enter_context(tc.tile_pool(name="rows", bufs=1))
+        work = ctx.enter_context(tc.tile_pool(name="work", bufs=CHUNKS))
+        flipped = ctx.enter_context(tc.psum_pool(name="flipped", bufs=4))
+        sums = ctx.enter_context(tc.psum_pool(name="sums", bufs=CHUNKS))
+
+        x_rows = rows.tile([P, IN], BF16)
+        nc.sync.dma_start(out=x_rows[:], in_=x2)
+        w_rows = []
+        for c in range(CHUNKS):
+            w_chunk = rows.tile([P, UNITS, W_PITCH], BF16, name="w_rows%d" % c)
+            nc.sync.dma_start(
+                out=w_chunk[:, :, 0 : IN + 1],
+                in_=weight[c * CHUNK : (c + 1) * CHUNK, :].rearrange("(j p) k -> p j k", p=P),
+            )
+            w_rows.append(w_chunk)
+
+        ident_f32 = const.tile([P, P], F32)
+        make_identity(nc, ident_f32[:])
+        ident_bf16 = const.tile([P, P], BF16)
+        make_identity(nc, ident_bf16[:])
+
+        warm = const.tile([P, 1], F32)
+        nc.vector.memset(warm[:], 0.0)
+        nc.scalar.activation(out=warm[:], in_=warm[:], func=ACT.Relu)
+
+        def quantise_rows(blocks, name):
+            n_rows = P * len(blocks)
+            half = PASSES * n_rows * PACK
+            grouped = work.tile([P, SIGNS * half], BF16, name=name + "_grouped", align_bytes=64)
+            words = grouped[:].bitcast(F32).rearrange(
+                "p (s g r u) -> p s g r u", s=SIGNS, g=PASSES, u=2
+            )
+            for j, block in enumerate(blocks):
+                flip_bank = flipped.tile([P, WORD_BLOCKS, P], F32, name="flip_bank")
+                block_words = block.bitcast(F32)
+                for m in range(WORD_BLOCKS):
+                    nc.tensor.transpose(flip_bank[:, m, :], block_words[:, m * P : (m + 1) * P], ident_f32[:])
+                nc.scalar.copy(
+                    out=words[:, 0, :, j * P : (j + 1) * P, :],
+                    in_=flip_bank[:].rearrange("p (g u) r -> p g r u", u=2),
+                )
+            ints = grouped[:].bitcast(I32)
+            nc.vector.tensor_scalar(
+                out=ints[:, half // 2 :],
+                in0=ints[:, : half // 2],
+                scalar1=CLEAR_SIGNS,
+                scalar2=None,
+                op0=ALU.bitwise_and,
+            )
+            codes = work.tile([P, SIGNS * PASSES * n_rows], U32, name=name + "_codes", align_bytes=64)
+            scales = work.tile([P, SIGNS * PASSES * n_rows], U8, name=name + "_scales", align_bytes=64)
+            nc.vector.quantize_mx(out=codes[:].bitcast(FP8X4), scales=scales[:], in_=grouped[:])
+            return codes, scales
+
+        x_codes, x_scales = quantise_rows([x_rows[:]], "x")
+
+        for c in range(CHUNKS):
+            w_chunk = w_rows[c]
+            sum_bank = sums.tile([P, 2 * CHUNK], F32, name="sum_bank")
+            w_codes, w_scales = quantise_rows([w_chunk[:, j, 0:IN] for j in range(UNITS)], "w")
+
+            for j in range(UNITS):
+                nc.tensor.matmul(
+                    out=sum_bank[:, j * P : (j + 1) * P],
+                    lhsT=w_chunk[:, j, IN : IN + 1].to_broadcast([P, P]),
+                    rhs=ident_bf16[:],
+                    start=True,
+                    stop=True,
+                )
+            bias = work.tile([P, CHUNK], F32, name="bias")
+            nc.scalar.activation(out=bias[:], in_=sum_bank[:, 0:CHUNK], func=ACT.Relu)
+
+            n_terms = SIGNS * PASSES
+            for i in range(n_terms):
+                nc.tensor.matmul_mx(
+                    out=sum_bank[:, CHUNK : 2 * CHUNK],
+                    lhsT=x_codes[:, i * P : (i + 1) * P].bitcast(FP8X4),
+                    lhsT_scale=x_scales[:, i * P : (i + 1) * P],
+                    rhs=w_codes[:, i * CHUNK : (i + 1) * CHUNK].bitcast(FP8X4),
+                    rhs_scale=w_scales[:, i * CHUNK : (i + 1) * CHUNK],
+                    start=(i == 0),
+                    stop=(i == n_terms - 1),
+                )
+
+            y = work.tile([P, CHUNK], F32, name="y")
+            nc.vector.scalar_tensor_tensor(
+                out=y[:],
+                in0=sum_bank[:, CHUNK : 2 * CHUNK],
+                scalar=0.5,
+                in1=bias[:],
+                op0=ALU.mult,
+                op1=ALU.add,
+            )
+            nc.sync.dma_start(out=out[:, c * CHUNK : (c + 1) * CHUNK], in_=y[:])

@@ -19,6 +19,7 @@ PACK = 4
 PASSES = IN // (P * PACK)
 WORD_BLOCKS = IN // 2 // P
 SIGNS = 2
+TERMS = SIGNS * PASSES
 UNITS = 2
 CHUNK = UNITS * P
 CHUNKS = OUT // CHUNK
@@ -30,25 +31,37 @@ FLOPS = 2 * 2 * P * IN * OUT
 
 def tile_skanlinear_s_kernel(tc, x, weight, out):
     nc = tc.nc
-    x2 = x.flatten_outer_dims()
 
     with ExitStack() as ctx:
         const = ctx.enter_context(tc.tile_pool(name="const", bufs=1))
-        rows = ctx.enter_context(tc.tile_pool(name="rows", bufs=1))
-        work = ctx.enter_context(tc.tile_pool(name="work", bufs=CHUNKS))
-        flipped = ctx.enter_context(tc.psum_pool(name="flipped", bufs=4))
+        keep = ctx.enter_context(tc.tile_pool(name="keep", bufs=1))
+        flipped = ctx.enter_context(tc.psum_pool(name="flipped", bufs=2 * UNITS))
         sums = ctx.enter_context(tc.psum_pool(name="sums", bufs=CHUNKS))
+        ctx.enter_context(tc.manual_schedule())
 
-        x_rows = rows.tile([P, IN], BF16)
-        nc.sync.dma_start(out=x_rows[:], in_=x2)
-        w_rows = []
+        def operand_tiles(name, n_rows):
+            n_words = TERMS * n_rows
+            return {
+                "grouped": keep.tile([P, n_words * PACK], BF16, name=name + "_grouped", align_bytes=64),
+                "codes": keep.tile([P, n_words], U32, name=name + "_codes", align_bytes=64),
+                "scales": keep.tile([P, n_words], U8, name=name + "_scales", align_bytes=64),
+            }
+
+        x_rows = keep.tile([P, 1, IN], BF16)
+        x_mx = operand_tiles("x", P)
+        w_rows = [keep.tile([P, UNITS, W_PITCH], BF16, name="w_rows%d" % c) for c in range(CHUNKS)]
+        w_mx = [operand_tiles("w%d" % c, CHUNK) for c in range(CHUNKS)]
+        bias = [keep.tile([P, CHUNK], F32, name="bias%d" % c) for c in range(CHUNKS)]
+        y = [keep.tile([P, CHUNK], F32, name="y%d" % c) for c in range(CHUNKS)]
+        sum_bank = [sums.tile([P, 2 * CHUNK], F32, name="sum_bank") for c in range(CHUNKS)]
+
+        nc.sync.dma_start(out=x_rows[:, 0, :], in_=x.flatten_outer_dims())
         for c in range(CHUNKS):
-            w_chunk = rows.tile([P, UNITS, W_PITCH], BF16, name="w_rows%d" % c)
-            nc.sync.dma_start(
-                out=w_chunk[:, :, 0 : IN + 1],
-                in_=weight[c * CHUNK : (c + 1) * CHUNK, :].rearrange("(j p) k -> p j k", p=P),
-            )
-            w_rows.append(w_chunk)
+            for j in range(UNITS):
+                first_row = c * CHUNK + j * P
+                nc.sync.dma_start(
+                    out=w_rows[c][:, j, 0 : IN + 1], in_=weight[first_row : first_row + P, :]
+                )
 
         ident_f32 = const.tile([P, P], F32)
         make_identity(nc, ident_f32[:])
@@ -59,72 +72,87 @@ def tile_skanlinear_s_kernel(tc, x, weight, out):
         nc.vector.memset(warm[:], 0.0)
         nc.scalar.activation(out=warm[:], in_=warm[:], func=ACT.Relu)
 
-        def quantise_rows(blocks, name):
-            n_rows = P * len(blocks)
-            half = PASSES * n_rows * PACK
-            grouped = work.tile([P, SIGNS * half], BF16, name=name + "_grouped", align_bytes=64)
-            words = grouped[:].bitcast(F32).rearrange(
+        def flip(rows, mx):
+            words = mx["grouped"][:].bitcast(F32).rearrange(
                 "p (s g r u) -> p s g r u", s=SIGNS, g=PASSES, u=2
             )
-            for j, block in enumerate(blocks):
+            for j in range(rows.shape[1]):
+                row_words = rows[:, j, 0:IN].bitcast(F32)
                 flip_bank = flipped.tile([P, WORD_BLOCKS, P], F32, name="flip_bank")
-                block_words = block.bitcast(F32)
                 for m in range(WORD_BLOCKS):
-                    nc.tensor.transpose(flip_bank[:, m, :], block_words[:, m * P : (m + 1) * P], ident_f32[:])
+                    nc.tensor.transpose(
+                        flip_bank[:, m, :], row_words[:, m * P : (m + 1) * P], ident_f32[:]
+                    )
                 nc.scalar.copy(
                     out=words[:, 0, :, j * P : (j + 1) * P, :],
                     in_=flip_bank[:].rearrange("p (g u) r -> p g r u", u=2),
                 )
-            ints = grouped[:].bitcast(I32)
-            nc.vector.tensor_scalar(
-                out=ints[:, half // 2 :],
-                in0=ints[:, : half // 2],
-                scalar1=CLEAR_SIGNS,
-                scalar2=None,
-                op0=ALU.bitwise_and,
-            )
-            codes = work.tile([P, SIGNS * PASSES * n_rows], U32, name=name + "_codes", align_bytes=64)
-            scales = work.tile([P, SIGNS * PASSES * n_rows], U8, name=name + "_scales", align_bytes=64)
-            nc.vector.quantize_mx(out=codes[:].bitcast(FP8X4), scales=scales[:], in_=grouped[:])
-            return codes, scales
 
-        x_codes, x_scales = quantise_rows([x_rows[:]], "x")
-
-        for c in range(CHUNKS):
-            w_chunk = w_rows[c]
-            sum_bank = sums.tile([P, 2 * CHUNK], F32, name="sum_bank")
-            w_codes, w_scales = quantise_rows([w_chunk[:, j, 0:IN] for j in range(UNITS)], "w")
-
+        def spread_bias(c):
             for j in range(UNITS):
                 nc.tensor.matmul(
-                    out=sum_bank[:, j * P : (j + 1) * P],
-                    lhsT=w_chunk[:, j, IN : IN + 1].to_broadcast([P, P]),
+                    out=sum_bank[c][:, j * P : (j + 1) * P],
+                    lhsT=w_rows[c][:, j, IN : IN + 1].to_broadcast([P, P]),
                     rhs=ident_bf16[:],
                     start=True,
                     stop=True,
                 )
-            bias = work.tile([P, CHUNK], F32, name="bias")
-            nc.scalar.activation(out=bias[:], in_=sum_bank[:, 0:CHUNK], func=ACT.Relu)
+            nc.scalar.activation(out=bias[c][:], in_=sum_bank[c][:, 0:CHUNK], func=ACT.Relu)
 
-            n_terms = SIGNS * PASSES
-            for i in range(n_terms):
+        def clear_signs(mx):
+            ints = mx["grouped"][:].bitcast(I32)
+            half = ints.shape[1] // SIGNS
+            nc.vector.tensor_scalar(
+                out=ints[:, half:],
+                in0=ints[:, :half],
+                scalar1=CLEAR_SIGNS,
+                scalar2=None,
+                op0=ALU.bitwise_and,
+            )
+
+        def quantise(mx):
+            nc.vector.quantize_mx(
+                out=mx["codes"][:].bitcast(FP8X4), scales=mx["scales"][:], in_=mx["grouped"][:]
+            )
+
+        def multiply(c):
+            for i in range(TERMS):
                 nc.tensor.matmul_mx(
-                    out=sum_bank[:, CHUNK : 2 * CHUNK],
-                    lhsT=x_codes[:, i * P : (i + 1) * P].bitcast(FP8X4),
-                    lhsT_scale=x_scales[:, i * P : (i + 1) * P],
-                    rhs=w_codes[:, i * CHUNK : (i + 1) * CHUNK].bitcast(FP8X4),
-                    rhs_scale=w_scales[:, i * CHUNK : (i + 1) * CHUNK],
+                    out=sum_bank[c][:, CHUNK : 2 * CHUNK],
+                    lhsT=x_mx["codes"][:, i * P : (i + 1) * P].bitcast(FP8X4),
+                    lhsT_scale=x_mx["scales"][:, i * P : (i + 1) * P],
+                    rhs=w_mx[c]["codes"][:, i * CHUNK : (i + 1) * CHUNK].bitcast(FP8X4),
+                    rhs_scale=w_mx[c]["scales"][:, i * CHUNK : (i + 1) * CHUNK],
                     start=(i == 0),
-                    stop=(i == n_terms - 1),
+                    stop=(i == TERMS - 1),
                 )
 
-            y = work.tile([P, CHUNK], F32, name="y")
+        def finish(c):
             nc.vector.scalar_tensor_tensor(
-                out=y[:],
-                in0=sum_bank[:, CHUNK : 2 * CHUNK],
+                out=y[c][:],
+                in0=sum_bank[c][:, CHUNK : 2 * CHUNK],
                 scalar=0.5,
-                in1=bias[:],
+                in1=bias[c][:],
                 op0=ALU.mult,
                 op1=ALU.add,
             )
-            nc.sync.dma_start(out=out[:, c * CHUNK : (c + 1) * CHUNK], in_=y[:])
+            nc.sync.dma_start(out=out[:, c * CHUNK : (c + 1) * CHUNK], in_=y[c][:])
+
+        flip(x_rows, x_mx)
+        clear_signs(x_mx)
+        quantise(x_mx)
+        for c in range(2):
+            flip(w_rows[c], w_mx[c])
+            spread_bias(c)
+        clear_signs(w_mx[0])
+        for c in range(CHUNKS + 1):
+            if c + 2 < CHUNKS:
+                flip(w_rows[c + 2], w_mx[c + 2])
+                spread_bias(c + 2)
+            if c + 1 < CHUNKS:
+                clear_signs(w_mx[c + 1])
+            if c < CHUNKS:
+                quantise(w_mx[c])
+                multiply(c)
+            if c >= 1:
+                finish(c - 1)

@@ -25,6 +25,7 @@ CHUNK = UNITS * P
 CHUNKS = OUT // CHUNK
 W_PITCH = 1040
 CLEAR_SIGNS = 0x7FFF7FFF
+LAG = 2
 
 FLOPS = 2 * 2 * P * IN * OUT
 
@@ -110,10 +111,19 @@ def tile_skanlinear_s_kernel(tc, x, weight, out):
                 op0=ALU.bitwise_and,
             )
 
-        def quantise(mx):
+        def quantise(mx, s):
+            n_words = mx["codes"].shape[1] // SIGNS
+            word_cols = slice(s * n_words, (s + 1) * n_words)
             nc.vector.quantize_mx(
-                out=mx["codes"][:].bitcast(FP8X4), scales=mx["scales"][:], in_=mx["grouped"][:]
+                out=mx["codes"][:, word_cols].bitcast(FP8X4),
+                scales=mx["scales"][:, word_cols],
+                in_=mx["grouped"][:, s * n_words * PACK : (s + 1) * n_words * PACK],
             )
+
+        def prepare(mx):
+            clear_signs(mx)
+            quantise(mx, 0)
+            quantise(mx, 1)
 
         def multiply(c):
             for i in range(TERMS):
@@ -139,20 +149,14 @@ def tile_skanlinear_s_kernel(tc, x, weight, out):
             nc.sync.dma_start(out=out[:, c * CHUNK : (c + 1) * CHUNK], in_=y[c][:])
 
         flip(x_rows, x_mx)
-        clear_signs(x_mx)
-        quantise(x_mx)
-        for c in range(2):
+        for c in range(CHUNKS):
             flip(w_rows[c], w_mx[c])
             spread_bias(c)
-        clear_signs(w_mx[0])
-        for c in range(CHUNKS + 1):
-            if c + 2 < CHUNKS:
-                flip(w_rows[c + 2], w_mx[c + 2])
-                spread_bias(c + 2)
-            if c + 1 < CHUNKS:
-                clear_signs(w_mx[c + 1])
-            if c < CHUNKS:
-                quantise(w_mx[c])
-                multiply(c)
-            if c >= 1:
-                finish(c - 1)
+        prepare(x_mx)
+        for c in range(CHUNKS):
+            prepare(w_mx[c])
+            multiply(c)
+            if c >= LAG:
+                finish(c - LAG)
+        for c in range(CHUNKS - LAG, CHUNKS):
+            finish(c)

@@ -71,12 +71,13 @@ def tile_skanlinear_s_kernel(tc, x, weight, out):
 
         warm = const.tile([P, 1], F32)
         nc.vector.memset(warm[:], 0.0)
-        nc.scalar.activation(out=warm[:], in_=warm[:], func=ACT.Relu)
+        nc.scalar.activation(out=warm[:], in_=warm[:], func=ACT.Abs)
 
         def flip(rows, mx):
             words = mx["grouped"][:].bitcast(F32).rearrange(
                 "p (s g r u) -> p s g r u", s=SIGNS, g=PASSES, u=2
             )
+            flip_banks = []
             for j in range(rows.shape[1]):
                 row_words = rows[:, j, 0:IN].bitcast(F32)
                 flip_bank = flipped.tile([P, WORD_BLOCKS, P], F32, name="flip_bank")
@@ -88,6 +89,8 @@ def tile_skanlinear_s_kernel(tc, x, weight, out):
                     out=words[:, 0, :, j * P : (j + 1) * P, :],
                     in_=flip_bank[:].rearrange("p (g u) r -> p g r u", u=2),
                 )
+                flip_banks.append(flip_bank)
+            return flip_banks
 
         def spread_bias(c):
             for j in range(UNITS):
@@ -99,6 +102,21 @@ def tile_skanlinear_s_kernel(tc, x, weight, out):
                     stop=True,
                 )
             nc.scalar.activation(out=bias[c][:], in_=sum_bank[c][:, 0:CHUNK], func=ACT.Relu)
+
+        def scalar_absolute(flip_banks, mx):
+            values = mx["grouped"][:].rearrange(
+                "p (s g r u e) -> p s g r u e", s=SIGNS, g=PASSES, u=2, e=2
+            )
+            for j, flip_bank in enumerate(flip_banks):
+                pairs = flip_bank[:].bitcast(BF16).rearrange(
+                    "p (g u) (r e) -> p g r u e", u=2, e=2
+                )
+                for g in range(PASSES):
+                    nc.scalar.activation(
+                        out=values[:, 1, g, j * P : (j + 1) * P, :, :],
+                        in_=pairs[:, g, :, :, :],
+                        func=ACT.Abs,
+                    )
 
         def clear_signs(mx):
             ints = mx["grouped"][:].bitcast(I32)
@@ -120,8 +138,9 @@ def tile_skanlinear_s_kernel(tc, x, weight, out):
                 in_=mx["grouped"][:, s * n_words * PACK : (s + 1) * n_words * PACK],
             )
 
-        def prepare(mx):
-            clear_signs(mx)
+        def prepare(mx, absolute_is_made):
+            if not absolute_is_made:
+                clear_signs(mx)
             quantise(mx, 0)
             quantise(mx, 1)
 
@@ -148,13 +167,16 @@ def tile_skanlinear_s_kernel(tc, x, weight, out):
             )
             nc.sync.dma_start(out=out[:, c * CHUNK : (c + 1) * CHUNK], in_=y[c][:])
 
+        last = CHUNKS - 1
         flip(x_rows, x_mx)
         for c in range(CHUNKS):
-            flip(w_rows[c], w_mx[c])
+            flip_banks = flip(w_rows[c], w_mx[c])
+            if c == last:
+                scalar_absolute(flip_banks, w_mx[c])
             spread_bias(c)
-        prepare(x_mx)
+        prepare(x_mx, False)
         for c in range(CHUNKS):
-            prepare(w_mx[c])
+            prepare(w_mx[c], c == last)
             multiply(c)
             if c >= LAG:
                 finish(c - LAG)

@@ -15,6 +15,7 @@ ACT = mybir.ActivationFunctionType
 P = 128
 IN = 1024
 OUT = 1024
+BANK = 512
 PACK = 4
 PASSES = IN // (P * PACK)
 WORD_BLOCKS = IN // 2 // P
@@ -25,7 +26,6 @@ CHUNK = UNITS * P
 CHUNKS = OUT // CHUNK
 W_PITCH = 1040
 CLEAR_SIGNS = 0x7FFF7FFF
-LAG = 2
 
 FLOPS = 2 * 2 * P * IN * OUT
 
@@ -37,7 +37,7 @@ def tile_skanlinear_s_kernel(tc, x, weight, out):
         const = ctx.enter_context(tc.tile_pool(name="const", bufs=1))
         keep = ctx.enter_context(tc.tile_pool(name="keep", bufs=1))
         flipped = ctx.enter_context(tc.psum_pool(name="flipped", bufs=2 * UNITS))
-        sums = ctx.enter_context(tc.psum_pool(name="sums", bufs=CHUNKS))
+        rows_out = ctx.enter_context(tc.psum_pool(name="rows_out", bufs=1))
         ctx.enter_context(tc.manual_schedule())
 
         def operand_tiles(name, n_rows):
@@ -52,9 +52,13 @@ def tile_skanlinear_s_kernel(tc, x, weight, out):
         x_mx = operand_tiles("x", P)
         w_rows = [keep.tile([P, UNITS, W_PITCH], BF16, name="w_rows%d" % c) for c in range(CHUNKS)]
         w_mx = [operand_tiles("w%d" % c, CHUNK) for c in range(CHUNKS)]
-        bias = [keep.tile([P, CHUNK], F32, name="bias%d" % c) for c in range(CHUNKS)]
+        bias = keep.tile([P, OUT], F32)
         y = [keep.tile([P, CHUNK], F32, name="y%d" % c) for c in range(CHUNKS)]
-        sum_bank = [sums.tile([P, 2 * CHUNK], F32, name="sum_bank") for c in range(CHUNKS)]
+        bias_banks = [rows_out.tile([P, BANK], F32, name="bias_bank%d" % b) for b in range(OUT // BANK)]
+        sum_banks = [rows_out.tile([P, BANK], F32, name="sum_bank%d" % b) for b in range(OUT // BANK)]
+
+        def in_bank(banks, first, width):
+            return banks[first // BANK][:, first % BANK : first % BANK + width]
 
         nc.sync.dma_start(out=x_rows[:, 0, :], in_=x.flatten_outer_dims())
         for c in range(CHUNKS):
@@ -92,16 +96,15 @@ def tile_skanlinear_s_kernel(tc, x, weight, out):
                 flip_banks.append(flip_bank)
             return flip_banks
 
-        def spread_bias(c):
+        def spread_wb(c):
             for j in range(UNITS):
                 nc.tensor.matmul(
-                    out=sum_bank[c][:, j * P : (j + 1) * P],
+                    out=in_bank(bias_banks, c * CHUNK + j * P, P),
                     lhsT=w_rows[c][:, j, IN : IN + 1].to_broadcast([P, P]),
                     rhs=ident_bf16[:],
                     start=True,
                     stop=True,
                 )
-            nc.scalar.activation(out=bias[c][:], in_=sum_bank[c][:, 0:CHUNK], func=ACT.Relu)
 
         def scalar_absolute(flip_banks, mx):
             values = mx["grouped"][:].rearrange(
@@ -138,16 +141,10 @@ def tile_skanlinear_s_kernel(tc, x, weight, out):
                 in_=mx["grouped"][:, s * n_words * PACK : (s + 1) * n_words * PACK],
             )
 
-        def prepare(mx, absolute_is_made):
-            if not absolute_is_made:
-                clear_signs(mx)
-            quantise(mx, 0)
-            quantise(mx, 1)
-
         def multiply(c):
             for i in range(TERMS):
                 nc.tensor.matmul_mx(
-                    out=sum_bank[c][:, CHUNK : 2 * CHUNK],
+                    out=in_bank(sum_banks, c * CHUNK, CHUNK),
                     lhsT=x_mx["codes"][:, i * P : (i + 1) * P].bitcast(FP8X4),
                     lhsT_scale=x_mx["scales"][:, i * P : (i + 1) * P],
                     rhs=w_mx[c]["codes"][:, i * CHUNK : (i + 1) * CHUNK].bitcast(FP8X4),
@@ -159,9 +156,9 @@ def tile_skanlinear_s_kernel(tc, x, weight, out):
         def finish(c):
             nc.vector.scalar_tensor_tensor(
                 out=y[c][:],
-                in0=sum_bank[c][:, CHUNK : 2 * CHUNK],
+                in0=in_bank(sum_banks, c * CHUNK, CHUNK),
                 scalar=0.5,
-                in1=bias[c][:],
+                in1=bias[:, c * CHUNK : (c + 1) * CHUNK],
                 op0=ALU.mult,
                 op1=ALU.add,
             )
@@ -169,16 +166,23 @@ def tile_skanlinear_s_kernel(tc, x, weight, out):
 
         last = CHUNKS - 1
         flip(x_rows, x_mx)
+        w_flipped = [flip(w_rows[c], w_mx[c]) for c in range(CHUNKS)]
+        scalar_absolute(w_flipped[last], w_mx[last])
         for c in range(CHUNKS):
-            flip_banks = flip(w_rows[c], w_mx[c])
-            if c == last:
-                scalar_absolute(flip_banks, w_mx[c])
-            spread_bias(c)
-        prepare(x_mx, False)
+            spread_wb(c)
+        for b, bias_bank in enumerate(bias_banks):
+            nc.scalar.activation(
+                out=bias[:, b * BANK : (b + 1) * BANK], in_=bias_bank[:], func=ACT.Relu
+            )
+
+        clear_signs(x_mx)
+        quantise(x_mx, 0)
+        quantise(x_mx, 1)
         for c in range(CHUNKS):
-            prepare(w_mx[c], c == last)
+            if c != last:
+                clear_signs(w_mx[c])
+            quantise(w_mx[c], 0)
+            quantise(w_mx[c], 1)
             multiply(c)
-            if c >= LAG:
-                finish(c - LAG)
-        for c in range(CHUNKS - LAG, CHUNKS):
+        for c in range(CHUNKS):
             finish(c)

from contextlib import ExitStack

import concourse.mybir as mybir
from concourse.masks import make_identity

F32 = mybir.dt.float32
BF16 = mybir.dt.bfloat16
I32 = mybir.dt.int32
U32 = mybir.dt.uint32
U8 = mybir.dt.uint8
FP8X4 = mybir.dt.float8_e4m3fn_x4
ALU = mybir.AluOpType
ACT = mybir.ActivationFunctionType

P = 128
IN = 1024
OUT = 1024
BANK = 512
PACK = 4
PASSES = IN // (P * PACK)
WORD_BLOCKS = IN // 2 // P
SIGNS = 2
TERMS = SIGNS * PASSES
UNITS = 2
CHUNK = UNITS * P
CHUNKS = OUT // CHUNK
W_PITCH = 1040
CLEAR_SIGNS = 0x7FFF7FFF

FLOPS = 2 * 2 * P * IN * OUT


def tile_skanlinear_s_kernel(tc, x, weight, out):
    nc = tc.nc

    with ExitStack() as ctx:
        const = ctx.enter_context(tc.tile_pool(name="const", bufs=1))
        keep = ctx.enter_context(tc.tile_pool(name="keep", bufs=1))
        flipped = ctx.enter_context(tc.psum_pool(name="flipped", bufs=2 * UNITS))
        rows_out = ctx.enter_context(tc.psum_pool(name="rows_out", bufs=1))
        ctx.enter_context(tc.manual_schedule())

        def operand_tiles(name, n_rows):
            n_words = TERMS * n_rows
            return {
                "grouped": keep.tile([P, n_words * PACK], BF16, name=name + "_grouped", align_bytes=64),
                "codes": keep.tile([P, n_words], U32, name=name + "_codes", align_bytes=64),
                "scales": keep.tile([P, n_words], U8, name=name + "_scales", align_bytes=64),
            }

        x_rows = keep.tile([P, 1, IN], BF16)
        x_mx = operand_tiles("x", P)
        w_rows = [keep.tile([P, UNITS, W_PITCH], BF16, name="w_rows%d" % c) for c in range(CHUNKS)]
        w_mx = [operand_tiles("w%d" % c, CHUNK) for c in range(CHUNKS)]
        bias = keep.tile([P, OUT], F32)
        y = [keep.tile([P, CHUNK], F32, name="y%d" % c) for c in range(CHUNKS)]
        bias_banks = [rows_out.tile([P, BANK], F32, name="bias_bank%d" % b) for b in range(OUT // BANK)]
        sum_banks = [rows_out.tile([P, BANK], F32, name="sum_bank%d" % b) for b in range(OUT // BANK)]

        def in_bank(banks, first, width):
            return banks[first // BANK][:, first % BANK : first % BANK + width]

        nc.sync.dma_start(out=x_rows[:, 0, :], in_=x.flatten_outer_dims())
        for c in range(CHUNKS):
            for j in range(UNITS):
                first_row = c * CHUNK + j * P
                nc.sync.dma_start(
                    out=w_rows[c][:, j, 0 : IN + 1], in_=weight[first_row : first_row + P, :]
                )

        ident_f32 = const.tile([P, P], F32)
        make_identity(nc, ident_f32[:])
        ident_bf16 = const.tile([P, P], BF16)
        make_identity(nc, ident_bf16[:])

        warm = const.tile([P, 1], F32)
        nc.vector.memset(warm[:], 0.0)
        nc.scalar.activation(out=warm[:], in_=warm[:], func=ACT.Abs)

        def flip(rows, mx):
            words = mx["grouped"][:].bitcast(F32).rearrange(
                "p (s g r u) -> p s g r u", s=SIGNS, g=PASSES, u=2
            )
            flip_banks = []
            for j in range(rows.shape[1]):
                row_words = rows[:, j, 0:IN].bitcast(F32)
                flip_bank = flipped.tile([P, WORD_BLOCKS, P], F32, name="flip_bank")
                for m in range(WORD_BLOCKS):
                    nc.tensor.transpose(
                        flip_bank[:, m, :], row_words[:, m * P : (m + 1) * P], ident_f32[:]
                    )
                nc.scalar.copy(
                    out=words[:, 0, :, j * P : (j + 1) * P, :],
                    in_=flip_bank[:].rearrange("p (g u) r -> p g r u", u=2),
                )
                flip_banks.append(flip_bank)
            return flip_banks

        def spread_wb(c):
            for j in range(UNITS):
                nc.tensor.matmul(
                    out=in_bank(bias_banks, c * CHUNK + j * P, P),
                    lhsT=w_rows[c][:, j, IN : IN + 1].to_broadcast([P, P]),
                    rhs=ident_bf16[:],
                    start=True,
                    stop=True,
                )

        def scalar_absolute(flip_banks, mx):
            values = mx["grouped"][:].rearrange(
                "p (s g r u e) -> p s g r u e", s=SIGNS, g=PASSES, u=2, e=2
            )
            for j, flip_bank in enumerate(flip_banks):
                pairs = flip_bank[:].bitcast(BF16).rearrange(
                    "p (g u) (r e) -> p g r u e", u=2, e=2
                )
                for g in range(PASSES):
                    nc.scalar.activation(
                        out=values[:, 1, g, j * P : (j + 1) * P, :, :],
                        in_=pairs[:, g, :, :, :],
                        func=ACT.Abs,
                    )

        def clear_signs(mx):
            ints = mx["grouped"][:].bitcast(I32)
            half = ints.shape[1] // SIGNS
            nc.vector.tensor_scalar(
                out=ints[:, half:],
                in0=ints[:, :half],
                scalar1=CLEAR_SIGNS,
                scalar2=None,
                op0=ALU.bitwise_and,
            )

        def quantise(mx, s):
            n_words = mx["codes"].shape[1] // SIGNS
            word_cols = slice(s * n_words, (s + 1) * n_words)
            nc.vector.quantize_mx(
                out=mx["codes"][:, word_cols].bitcast(FP8X4),
                scales=mx["scales"][:, word_cols],
                in_=mx["grouped"][:, s * n_words * PACK : (s + 1) * n_words * PACK],
            )

        def multiply(c):
            for i in range(TERMS):
                nc.tensor.matmul_mx(
                    out=in_bank(sum_banks, c * CHUNK, CHUNK),
                    lhsT=x_mx["codes"][:, i * P : (i + 1) * P].bitcast(FP8X4),
                    lhsT_scale=x_mx["scales"][:, i * P : (i + 1) * P],
                    rhs=w_mx[c]["codes"][:, i * CHUNK : (i + 1) * CHUNK].bitcast(FP8X4),
                    rhs_scale=w_mx[c]["scales"][:, i * CHUNK : (i + 1) * CHUNK],
                    start=(i == 0),
                    stop=(i == TERMS - 1),
                )

        def finish(c):
            nc.vector.scalar_tensor_tensor(
                out=y[c][:],
                in0=in_bank(sum_banks, c * CHUNK, CHUNK),
                scalar=0.5,
                in1=bias[:, c * CHUNK : (c + 1) * CHUNK],
                op0=ALU.mult,
                op1=ALU.add,
            )
            nc.sync.dma_start(out=out[:, c * CHUNK : (c + 1) * CHUNK], in_=y[c][:])

        last = CHUNKS - 1
        flip(x_rows, x_mx)
        w_flipped = [flip(w_rows[c], w_mx[c]) for c in range(CHUNKS)]
        scalar_absolute(w_flipped[last], w_mx[last])
        for c in range(CHUNKS):
            spread_wb(c)
        for b, bias_bank in enumerate(bias_banks):
            nc.scalar.activation(
                out=bias[:, b * BANK : (b + 1) * BANK], in_=bias_bank[:], func=ACT.Relu
            )

        clear_signs(x_mx)
        quantise(x_mx, 0)
        quantise(x_mx, 1)
        for c in range(CHUNKS):
            if c != last:
                clear_signs(w_mx[c])
            quantise(w_mx[c], 0)
            quantise(w_mx[c], 1)
            multiply(c)
        for c in range(CHUNKS):
            finish(c)
